import numpy as np
import ml_dtypes

BF16 = ml_dtypes.bfloat16


def bf(x):
    return np.asarray(x, np.float32).astype(BF16)


def f32(x):
    return np.asarray(x, np.float32)


def f64(x):
    return np.asarray(x).astype(np.float64)


def striped(idx):
    return np.tile(idx.reshape(-1, 16).T, (8, 1))


KVH, D, D2, HID, C, S, N = 4, 128, 64, 512, 512, 2048, 256


def setup_inputs():
    return {
        "x": bf(np.random.standard_normal((HID, N))),
        "w_k": bf(np.random.standard_normal((HID, C)) / np.sqrt(HID)),
        "b_k": f32(0.3 * np.random.standard_normal((C, 1))),
        "cos": f32(np.random.uniform(-1.0, 1.0, (D2, N))),
        "sin": f32(np.random.uniform(-1.0, 1.0, (D2, N))),
        "base": f32(np.random.standard_normal((C, S))),
        "offs": striped(np.random.permutation(S)[:N]),
    }


def reference(x, w_k, b_k, cos, sin, base, offs):
    idx = offs[:16].T.reshape(-1)
    kp = (f64(w_k).T @ f64(x) + f64(b_k)).reshape(KVH, D, N)
    k1, k2 = kp[:, :D2], kp[:, D2:]
    cc, ss = f64(cos)[None], f64(sin)[None]
    rot = np.concatenate([k1 * cc - k2 * ss, k2 * cc + k1 * ss], axis=1).reshape(C, N)
    res = f64(base).copy()
    res[:, idx] = rot
    return res

@@ -1,0 +1,104 @@
+import concourse.mybir as mybir
+from concourse.masks import make_identity
+
+FP32 = mybir.dt.float32
+BF16 = mybir.dt.bfloat16
+U16 = mybir.dt.uint16
+ADD = mybir.AluOpType.add
+MULT = mybir.AluOpType.mult
+
+P = 128
+HALF = 64
+HEADS = 4
+HIDDEN = 512
+K_STEPS = HIDDEN // P
+CHANNELS = HEADS * P
+TOKENS = 256
+SLOTS = 2048
+
+FLOPS = 2 * HIDDEN * CHANNELS * TOKENS
+
+
+def tile_flashshellattention_kernel(tc, x, w_k, b_k, cos, sin, base, offs, out):
+    nc = tc.nc
+    with (
+        tc.tile_pool(name="held", bufs=1) as held,
+        tc.tile_pool(name="products", bufs=2) as products,
+        tc.psum_pool(name="spread", bufs=1) as spread,
+        tc.psum_pool(name="projections", bufs=2) as projections,
+    ):
+        offsets = held.tile([P, TOKENS // 16], U16, name="offsets")
+        nc.sync.dma_start(offsets[:], offs)
+
+        x_sb = held.tile([P, K_STEPS, TOKENS], BF16, name="x_sb")
+        nc.sync.dma_start(x_sb[:], x.rearrange("(p k) n -> p k n", k=K_STEPS))
+        w_own = held.tile([P, K_STEPS, CHANNELS], BF16, name="w_own")
+        nc.sync.dma_start(w_own[:], w_k.rearrange("(p k) c -> p k c", k=K_STEPS))
+
+        cos_both = held.tile([P, TOKENS], FP32, name="cos_both")
+        signed_sin = held.tile([P, TOKENS], FP32, name="signed_sin")
+        for lower in (0, HALF):
+            nc.scalar.dma_start(cos_both[lower : lower + HALF, :], cos)
+            nc.scalar.dma_start(signed_sin[lower : lower + HALF, :], sin)
+
+        bias_rows = held.tile([2 * HEADS, P], FP32, name="bias_rows")
+        nc.gpsimd.dma_start(bias_rows[0:HEADS, :], b_k.rearrange("(h c) o -> h (c o)", c=P))
+        b_halves = b_k.rearrange("(h t d) o -> h t (d o)", t=2, d=HALF)
+        for t in range(2):
+            nc.gpsimd.dma_start(
+                bias_rows[HEADS : 2 * HEADS, t * HALF : (t + 1) * HALF], b_halves[:, 1 - t, :]
+            )
+
+        windows = []
+        for h in range(HEADS):
+            window = held.tile([P, SLOTS], FP32, name=f"window{h}")
+            nc.sync.dma_start(window[:], base[h * P : (h + 1) * P, :])
+            windows.append(window)
+
+        nc.vector.tensor_scalar_mul(signed_sin[0:HALF, :], signed_sin[0:HALF, :], -1.0)
+
+        w_partner = held.tile([P, K_STEPS, CHANNELS], BF16, name="w_partner")
+        own_halves = w_own[:].rearrange("p k (h t d) -> p k h t d", t=2, d=HALF)
+        partner_halves = w_partner[:].rearrange("p k (h t d) -> p k h t d", t=2, d=HALF)
+        for t in range(2):
+            nc.vector.tensor_copy(partner_halves[:, :, :, t, :], own_halves[:, :, :, 1 - t, :])
+
+        identity = held.tile([2 * HEADS, 2 * HEADS], FP32, name="identity")
+        make_identity(nc, identity[:])
+        bias_ps = spread.tile([P, 2 * HEADS], FP32, name="bias_ps")
+        nc.tensor.matmul(bias_ps[:], lhsT=bias_rows[:], rhs=identity[:], start=True, stop=True)
+        bias = held.tile([P, 2 * HEADS], FP32, name="bias")
+        nc.vector.tensor_copy(bias[:], bias_ps[:])
+
+        for h in range(HEADS):
+            head = slice(h * P, (h + 1) * P)
+            own_ps = projections.tile([P, TOKENS], FP32, name="own_ps")
+            partner_ps = projections.tile([P, TOKENS], FP32, name="partner_ps")
+            for psum, weights in ((own_ps, w_own), (partner_ps, w_partner)):
+                for k in range(K_STEPS):
+                    nc.tensor.matmul(
+                        psum[:],
+                        lhsT=weights[:, k, head],
+                        rhs=x_sb[:, k, :],
+                        start=(k == 0),
+                        stop=(k == K_STEPS - 1),
+                    )
+
+            cos_part = products.tile([P, TOKENS], FP32, name="cos_part")
+            nc.vector.scalar_tensor_tensor(
+                cos_part[:], own_ps[:], bias[:, h : h + 1], cos_both[:], op0=ADD, op1=MULT
+            )
+            sin_part = products.tile([P, TOKENS], FP32, name="sin_part")
+            nc.vector.scalar_tensor_tensor(
+                sin_part[:],
+                partner_ps[:],
+                bias[:, HEADS + h : HEADS + h + 1],
+                signed_sin[:],
+                op0=ADD,
+                op1=MULT,
+            )
+
+            nc.vector.tensor_tensor(
+                windows[h][:].indirect(offsets[:]), cos_part[:], sin_part[:], ADD
+            )
+            nc.scalar.dma_start(out[head, :], windows[h][:])

@@ -35,19 +35,19 @@ def tile_flashshellattention_kernel(tc, x, w_k, b_k, cos, sin, base, offs, out):
         w_own = held.tile([P, K_STEPS, CHANNELS], BF16, name="w_own")
         nc.sync.dma_start(w_own[:], w_k.rearrange("(p k) c -> p k c", k=K_STEPS))
 
+        bias_rows = held.tile([2 * HEADS, P], FP32, name="bias_rows")
+        nc.scalar.dma_start(bias_rows[0:HEADS, :], b_k.rearrange("(h c) o -> h (c o)", c=P))
+        b_halves = b_k.rearrange("(h t d) o -> h t (d o)", t=2, d=HALF)
+        for t in range(2):
+            nc.scalar.dma_start(
+                bias_rows[HEADS : 2 * HEADS, t * HALF : (t + 1) * HALF], b_halves[:, 1 - t, :]
+            )
+
         cos_both = held.tile([P, TOKENS], FP32, name="cos_both")
         signed_sin = held.tile([P, TOKENS], FP32, name="signed_sin")
         for lower in (0, HALF):
             nc.scalar.dma_start(cos_both[lower : lower + HALF, :], cos)
             nc.scalar.dma_start(signed_sin[lower : lower + HALF, :], sin)
-
-        bias_rows = held.tile([2 * HEADS, P], FP32, name="bias_rows")
-        nc.gpsimd.dma_start(bias_rows[0:HEADS, :], b_k.rearrange("(h c) o -> h (c o)", c=P))
-        b_halves = b_k.rearrange("(h t d) o -> h t (d o)", t=2, d=HALF)
-        for t in range(2):
-            nc.gpsimd.dma_start(
-                bias_rows[HEADS : 2 * HEADS, t * HALF : (t + 1) * HALF], b_halves[:, 1 - t, :]
-            )
 
         windows = []
         for h in range(HEADS):

@@ -35,13 +35,8 @@ def tile_flashshellattention_kernel(tc, x, w_k, b_k, cos, sin, base, offs, out):
         w_own = held.tile([P, K_STEPS, CHANNELS], BF16, name="w_own")
         nc.sync.dma_start(w_own[:], w_k.rearrange("(p k) c -> p k c", k=K_STEPS))
 
-        bias_rows = held.tile([2 * HEADS, P], FP32, name="bias_rows")
-        nc.scalar.dma_start(bias_rows[0:HEADS, :], b_k.rearrange("(h c) o -> h (c o)", c=P))
-        b_halves = b_k.rearrange("(h t d) o -> h t (d o)", t=2, d=HALF)
-        for t in range(2):
-            nc.scalar.dma_start(
-                bias_rows[HEADS : 2 * HEADS, t * HALF : (t + 1) * HALF], b_halves[:, 1 - t, :]
-            )
+        bias_rows = held.tile([HEADS, P + HALF], FP32, name="bias_rows")
+        nc.scalar.dma_start(bias_rows[:, 0:P], b_k.rearrange("(h c) o -> h (c o)", c=P))
 
         cos_both = held.tile([P, TOKENS], FP32, name="cos_both")
         signed_sin = held.tile([P, TOKENS], FP32, name="signed_sin")
@@ -55,6 +50,23 @@ def tile_flashshellattention_kernel(tc, x, w_k, b_k, cos, sin, base, offs, out):
             nc.sync.dma_start(window[:], base[h * P : (h + 1) * P, :])
             windows.append(window)
 
+        nc.vector.tensor_copy(bias_rows[:, P : P + HALF], bias_rows[:, 0:HALF])
+        identity = held.tile([HEADS, HEADS], FP32, name="identity")
+        make_identity(nc, identity[:])
+        bias_ps = spread.tile([P, 2 * HEADS], FP32, name="bias_ps")
+        nc.tensor.matmul(
+            bias_ps[:, 0:HEADS], lhsT=bias_rows[:, 0:P], rhs=identity[:], start=True, stop=True
+        )
+        nc.tensor.matmul(
+            bias_ps[:, HEADS : 2 * HEADS],
+            lhsT=bias_rows[:, HALF : HALF + P],
+            rhs=identity[:],
+            start=True,
+            stop=True,
+        )
+        bias = held.tile([P, 2 * HEADS], FP32, name="bias")
+        nc.vector.tensor_copy(bias[:], bias_ps[:])
+
         nc.vector.tensor_scalar_mul(signed_sin[0:HALF, :], signed_sin[0:HALF, :], -1.0)
 
         w_partner = held.tile([P, K_STEPS, CHANNELS], BF16, name="w_partner")
@@ -62,13 +74,6 @@ def tile_flashshellattention_kernel(tc, x, w_k, b_k, cos, sin, base, offs, out):
         partner_halves = w_partner[:].rearrange("p k (h t d) -> p k h t d", t=2, d=HALF)
         for t in range(2):
             nc.vector.tensor_copy(partner_halves[:, :, :, t, :], own_halves[:, :, :, 1 - t, :])
-
-        identity = held.tile([2 * HEADS, 2 * HEADS], FP32, name="identity")
-        make_identity(nc, identity[:])
-        bias_ps = spread.tile([P, 2 * HEADS], FP32, name="bias_ps")
-        nc.tensor.matmul(bias_ps[:], lhsT=bias_rows[:], rhs=identity[:], start=True, stop=True)
-        bias = held.tile([P, 2 * HEADS], FP32, name="bias")
-        nc.vector.tensor_copy(bias[:], bias_ps[:])
 
         for h in range(HEADS):
             head = slice(h * P, (h + 1) * P)

@@ -15,6 +15,8 @@ K_STEPS = HIDDEN // P
 CHANNELS = HEADS * P
 TOKENS = 256
 SLOTS = 2048
+BANK = 512
+WARM_UP_MATMULS = 8
 
 FLOPS = 2 * HIDDEN * CHANNELS * TOKENS
 
@@ -49,6 +51,12 @@ def tile_flashshellattention_kernel(tc, x, w_k, b_k, cos, sin, base, offs, out):
             window = held.tile([P, SLOTS], FP32, name=f"window{h}")
             nc.sync.dma_start(window[:], base[h * P : (h + 1) * P, :])
             windows.append(window)
+
+        zeros = held.tile([P, BANK], BF16, name="zeros")
+        nc.vector.memset(zeros[:], 0.0)
+        unused_ps = spread.tile([P, BANK], FP32, name="unused_ps")
+        for step in range(WARM_UP_MATMULS):
+            nc.tensor.matmul(unused_ps[:], lhsT=zeros[:, 0:P], rhs=zeros[:], start=True, stop=True)
 
         nc.vector.tensor_copy(bias_rows[:, P : P + HALF], bias_rows[:, 0:HALF])
         identity = held.tile([HEADS, HEADS], FP32, name="identity")

@@ -15,8 +15,6 @@ K_STEPS = HIDDEN // P
 CHANNELS = HEADS * P
 TOKENS = 256
 SLOTS = 2048
-BANK = 512
-WARM_UP_MATMULS = 8
 
 FLOPS = 2 * HIDDEN * CHANNELS * TOKENS
 
@@ -32,31 +30,25 @@ def tile_flashshellattention_kernel(tc, x, w_k, b_k, cos, sin, base, offs, out):
         offsets = held.tile([P, TOKENS // 16], U16, name="offsets")
         nc.sync.dma_start(offsets[:], offs)
 
+        bias_rows = held.tile([HEADS, P + HALF], FP32, name="bias_rows")
+        nc.scalar.dma_start(bias_rows[:, 0:P], b_k.rearrange("(h c) o -> h (c o)", c=P))
+
         x_sb = held.tile([P, K_STEPS, TOKENS], BF16, name="x_sb")
         nc.sync.dma_start(x_sb[:], x.rearrange("(p k) n -> p k n", k=K_STEPS))
         w_own = held.tile([P, K_STEPS, CHANNELS], BF16, name="w_own")
         nc.sync.dma_start(w_own[:], w_k.rearrange("(p k) c -> p k c", k=K_STEPS))
 
-        bias_rows = held.tile([HEADS, P + HALF], FP32, name="bias_rows")
-        nc.scalar.dma_start(bias_rows[:, 0:P], b_k.rearrange("(h c) o -> h (c o)", c=P))
-
         cos_both = held.tile([P, TOKENS], FP32, name="cos_both")
         signed_sin = held.tile([P, TOKENS], FP32, name="signed_sin")
+        windows = [held.tile([P, SLOTS], FP32, name=f"window{h}") for h in range(HEADS)]
         for lower in (0, HALF):
             nc.scalar.dma_start(cos_both[lower : lower + HALF, :], cos)
+        for h in (0, 1):
+            nc.sync.dma_start(windows[h][:], base[h * P : (h + 1) * P, :])
+        for lower in (0, HALF):
             nc.scalar.dma_start(signed_sin[lower : lower + HALF, :], sin)
-
-        windows = []
-        for h in range(HEADS):
-            window = held.tile([P, SLOTS], FP32, name=f"window{h}")
-            nc.sync.dma_start(window[:], base[h * P : (h + 1) * P, :])
-            windows.append(window)
-
-        zeros = held.tile([P, BANK], BF16, name="zeros")
-        nc.vector.memset(zeros[:], 0.0)
-        unused_ps = spread.tile([P, BANK], FP32, name="unused_ps")
-        for step in range(WARM_UP_MATMULS):
-            nc.tensor.matmul(unused_ps[:], lhsT=zeros[:, 0:P], rhs=zeros[:], start=True, stop=True)
+        for h in (2, 3):
+            nc.sync.dma_start(windows[h][:], base[h * P : (h + 1) * P, :])
 
         nc.vector.tensor_copy(bias_rows[:, P : P + HALF], bias_rows[:, 0:HALF])
         identity = held.tile([HEADS, HEADS], FP32, name="identity")

@@ -15,6 +15,8 @@ K_STEPS = HIDDEN // P
 CHANNELS = HEADS * P
 TOKENS = 256
 SLOTS = 2048
+BANK = 512
+WARM_UP_MATMULS = 8
 
 FLOPS = 2 * HIDDEN * CHANNELS * TOKENS
 
@@ -49,6 +51,12 @@ def tile_flashshellattention_kernel(tc, x, w_k, b_k, cos, sin, base, offs, out):
             nc.scalar.dma_start(signed_sin[lower : lower + HALF, :], sin)
         for h in (2, 3):
             nc.sync.dma_start(windows[h][:], base[h * P : (h + 1) * P, :])
+
+        zeros = held.tile([P, BANK], BF16, name="zeros")
+        nc.vector.memset(zeros[:], 0.0)
+        unused_ps = spread.tile([P, BANK], FP32, name="unused_ps")
+        for step in range(WARM_UP_MATMULS):
+            nc.tensor.matmul(unused_ps[:], lhsT=zeros[:, 0:P], rhs=zeros[:], start=True, stop=True)
 
         nc.vector.tensor_copy(bias_rows[:, P : P + HALF], bias_rows[:, 0:HALF])
         identity = held.tile([HEADS, HEADS], FP32, name="identity")

@@ -15,8 +15,6 @@ K_STEPS = HIDDEN // P
 CHANNELS = HEADS * P
 TOKENS = 256
 SLOTS = 2048
-BANK = 512
-WARM_UP_MATMULS = 8
 
 FLOPS = 2 * HIDDEN * CHANNELS * TOKENS
 
@@ -43,20 +41,15 @@ def tile_flashshellattention_kernel(tc, x, w_k, b_k, cos, sin, base, offs, out):
         cos_both = held.tile([P, TOKENS], FP32, name="cos_both")
         signed_sin = held.tile([P, TOKENS], FP32, name="signed_sin")
         windows = [held.tile([P, SLOTS], FP32, name=f"window{h}") for h in range(HEADS)]
+        window_queues = [nc.sync, nc.scalar, nc.sync, nc.scalar]
         for lower in (0, HALF):
             nc.scalar.dma_start(cos_both[lower : lower + HALF, :], cos)
         for h in (0, 1):
-            nc.sync.dma_start(windows[h][:], base[h * P : (h + 1) * P, :])
+            window_queues[h].dma_start(windows[h][:], base[h * P : (h + 1) * P, :])
         for lower in (0, HALF):
             nc.scalar.dma_start(signed_sin[lower : lower + HALF, :], sin)
         for h in (2, 3):
-            nc.sync.dma_start(windows[h][:], base[h * P : (h + 1) * P, :])
-
-        zeros = held.tile([P, BANK], BF16, name="zeros")
-        nc.vector.memset(zeros[:], 0.0)
-        unused_ps = spread.tile([P, BANK], FP32, name="unused_ps")
-        for step in range(WARM_UP_MATMULS):
-            nc.tensor.matmul(unused_ps[:], lhsT=zeros[:, 0:P], rhs=zeros[:], start=True, stop=True)
+            window_queues[h].dma_start(windows[h][:], base[h * P : (h + 1) * P, :])
 
         nc.vector.tensor_copy(bias_rows[:, P : P + HALF], bias_rows[:, 0:HALF])
         identity = held.tile([HEADS, HEADS], FP32, name="identity")
@@ -114,4 +107,4 @@ def tile_flashshellattention_kernel(tc, x, w_k, b_k, cos, sin, base, offs, out):
             nc.vector.tensor_tensor(
                 windows[h][:].indirect(offsets[:]), cos_part[:], sin_part[:], ADD
             )
-            nc.scalar.dma_start(out[head, :], windows[h][:])
+            window_queues[h].dma_start(out[head, :], windows[h][:])

@@ -41,15 +41,14 @@ def tile_flashshellattention_kernel(tc, x, w_k, b_k, cos, sin, base, offs, out):
         cos_both = held.tile([P, TOKENS], FP32, name="cos_both")
         signed_sin = held.tile([P, TOKENS], FP32, name="signed_sin")
         windows = [held.tile([P, SLOTS], FP32, name=f"window{h}") for h in range(HEADS)]
-        window_queues = [nc.sync, nc.scalar, nc.sync, nc.scalar]
         for lower in (0, HALF):
             nc.scalar.dma_start(cos_both[lower : lower + HALF, :], cos)
         for h in (0, 1):
-            window_queues[h].dma_start(windows[h][:], base[h * P : (h + 1) * P, :])
+            nc.sync.dma_start(windows[h][:], base[h * P : (h + 1) * P, :])
         for lower in (0, HALF):
             nc.scalar.dma_start(signed_sin[lower : lower + HALF, :], sin)
         for h in (2, 3):
-            window_queues[h].dma_start(windows[h][:], base[h * P : (h + 1) * P, :])
+            nc.sync.dma_start(windows[h][:], base[h * P : (h + 1) * P, :])
 
         nc.vector.tensor_copy(bias_rows[:, P : P + HALF], bias_rows[:, 0:HALF])
         identity = held.tile([HEADS, HEADS], FP32, name="identity")
@@ -107,4 +106,4 @@ def tile_flashshellattention_kernel(tc, x, w_k, b_k, cos, sin, base, offs, out):
             nc.vector.tensor_tensor(
                 windows[h][:].indirect(offsets[:]), cos_part[:], sin_part[:], ADD
             )
-            window_queues[h].dma_start(out[head, :], windows[h][:])
+            nc.sync.dma_start(out[head, :], windows[h][:])

@@ -38,36 +38,44 @@ def tile_flashshellattention_kernel(tc, x, w_k, b_k, cos, sin, base, offs, out):
         w_own = held.tile([P, K_STEPS, CHANNELS], BF16, name="w_own")
         nc.sync.dma_start(w_own[:], w_k.rearrange("(p k) c -> p k c", k=K_STEPS))
 
-        cos_both = held.tile([P, TOKENS], FP32, name="cos_both")
-        signed_sin = held.tile([P, TOKENS], FP32, name="signed_sin")
+        tables = held.tile([P, TOKENS], FP32, name="tables")
+        nc.scalar.dma_start(tables[0:HALF, :], cos)
+        nc.scalar.dma_start(tables[HALF:P, :], sin)
         windows = [held.tile([P, SLOTS], FP32, name=f"window{h}") for h in range(HEADS)]
-        for lower in (0, HALF):
-            nc.scalar.dma_start(cos_both[lower : lower + HALF, :], cos)
-        for h in (0, 1):
-            nc.sync.dma_start(windows[h][:], base[h * P : (h + 1) * P, :])
-        for lower in (0, HALF):
-            nc.scalar.dma_start(signed_sin[lower : lower + HALF, :], sin)
-        for h in (2, 3):
+        for h in range(HEADS):
             nc.sync.dma_start(windows[h][:], base[h * P : (h + 1) * P, :])
 
         nc.vector.tensor_copy(bias_rows[:, P : P + HALF], bias_rows[:, 0:HALF])
-        identity = held.tile([HEADS, HEADS], FP32, name="identity")
+        identity = held.tile([P, P], FP32, name="identity")
         make_identity(nc, identity[:])
         bias_ps = spread.tile([P, 2 * HEADS], FP32, name="bias_ps")
         nc.tensor.matmul(
-            bias_ps[:, 0:HEADS], lhsT=bias_rows[:, 0:P], rhs=identity[:], start=True, stop=True
+            bias_ps[:, 0:HEADS], lhsT=bias_rows[:, 0:P], rhs=identity[0:HEADS, 0:HEADS], start=True, stop=True
         )
         nc.tensor.matmul(
             bias_ps[:, HEADS : 2 * HEADS],
             lhsT=bias_rows[:, HALF : HALF + P],
-            rhs=identity[:],
+            rhs=identity[0:HEADS, 0:HEADS],
             start=True,
             stop=True,
         )
         bias = held.tile([P, 2 * HEADS], FP32, name="bias")
         nc.vector.tensor_copy(bias[:], bias_ps[:])
 
-        nc.vector.tensor_scalar_mul(signed_sin[0:HALF, :], signed_sin[0:HALF, :], -1.0)
+        spread_cos = held.tile([P, P], FP32, name="spread_cos")
+        spread_sin = held.tile([P, P], FP32, name="spread_sin")
+        nc.vector.tensor_copy(spread_cos[:, 0:HALF], identity[:, 0:HALF])
+        nc.vector.tensor_copy(spread_cos[:, HALF:P], identity[:, 0:HALF])
+        nc.vector.tensor_scalar_mul(spread_sin[:, 0:HALF], identity[:, HALF:P], -1.0)
+        nc.vector.tensor_copy(spread_sin[:, HALF:P], identity[:, HALF:P])
+        cos_ps = spread.tile([P, TOKENS], FP32, name="cos_ps")
+        nc.tensor.matmul(cos_ps[:], lhsT=spread_cos[:], rhs=tables[:], start=True, stop=True)
+        sin_ps = spread.tile([P, TOKENS], FP32, name="sin_ps")
+        nc.tensor.matmul(sin_ps[:], lhsT=spread_sin[:], rhs=tables[:], start=True, stop=True)
+        cos_both = held.tile([P, TOKENS], FP32, name="cos_both")
+        nc.scalar.copy(cos_both[:], cos_ps[:])
+        signed_sin = held.tile([P, TOKENS], FP32, name="signed_sin")
+        nc.scalar.copy(signed_sin[:], sin_ps[:])
 
         w_partner = held.tile([P, K_STEPS, CHANNELS], BF16, name="w_partner")
         own_halves = w_own[:].rearrange("p k (h t d) -> p k h t d", t=2, d=HALF)

@@ -14,6 +14,8 @@ HIDDEN = 512
 K_STEPS = HIDDEN // P
 CHANNELS = HEADS * P
 TOKENS = 256
+CUTS = 2
+CUT_TOKENS = TOKENS // CUTS
 SLOTS = 2048
 
 FLOPS = 2 * HIDDEN * CHANNELS * TOKENS
@@ -24,11 +26,14 @@ def tile_flashshellattention_kernel(tc, x, w_k, b_k, cos, sin, base, offs, out):
     with (
         tc.tile_pool(name="held", bufs=1) as held,
         tc.tile_pool(name="products", bufs=2) as products,
-        tc.psum_pool(name="spread", bufs=1) as spread,
-        tc.psum_pool(name="projections", bufs=2) as projections,
     ):
         offsets = held.tile([P, TOKENS // 16], U16, name="offsets")
         nc.sync.dma_start(offsets[:], offs)
+
+        cos_cut = held.tile([P, CUT_TOKENS], FP32, name="cos_cut")
+        nc.sync.dma_start(cos_cut[:], cos.rearrange("d (t n) -> (d t) n", t=CUTS))
+        sin_cut = held.tile([P, CUT_TOKENS], FP32, name="sin_cut")
+        nc.sync.dma_start(sin_cut[:], sin.rearrange("d (t n) -> (d t) n", t=CUTS))
 
         bias_rows = held.tile([HEADS, P + HALF], FP32, name="bias_rows")
         nc.scalar.dma_start(bias_rows[:, 0:P], b_k.rearrange("(h c) o -> h (c o)", c=P))
@@ -38,44 +43,49 @@ def tile_flashshellattention_kernel(tc, x, w_k, b_k, cos, sin, base, offs, out):
         w_own = held.tile([P, K_STEPS, CHANNELS], BF16, name="w_own")
         nc.sync.dma_start(w_own[:], w_k.rearrange("(p k) c -> p k c", k=K_STEPS))
 
-        tables = held.tile([P, TOKENS], FP32, name="tables")
-        nc.scalar.dma_start(tables[0:HALF, :], cos)
-        nc.scalar.dma_start(tables[HALF:P, :], sin)
         windows = [held.tile([P, SLOTS], FP32, name=f"window{h}") for h in range(HEADS)]
         for h in range(HEADS):
             nc.sync.dma_start(windows[h][:], base[h * P : (h + 1) * P, :])
 
-        nc.vector.tensor_copy(bias_rows[:, P : P + HALF], bias_rows[:, 0:HALF])
         identity = held.tile([P, P], FP32, name="identity")
         make_identity(nc, identity[:])
-        bias_ps = spread.tile([P, 2 * HEADS], FP32, name="bias_ps")
-        nc.tensor.matmul(
-            bias_ps[:, 0:HEADS], lhsT=bias_rows[:, 0:P], rhs=identity[0:HEADS, 0:HEADS], start=True, stop=True
-        )
-        nc.tensor.matmul(
-            bias_ps[:, HEADS : 2 * HEADS],
-            lhsT=bias_rows[:, HALF : HALF + P],
-            rhs=identity[0:HEADS, 0:HEADS],
-            start=True,
-            stop=True,
-        )
-        bias = held.tile([P, 2 * HEADS], FP32, name="bias")
-        nc.vector.tensor_copy(bias[:], bias_ps[:])
 
-        spread_cos = held.tile([P, P], FP32, name="spread_cos")
-        spread_sin = held.tile([P, P], FP32, name="spread_sin")
-        nc.vector.tensor_copy(spread_cos[:, 0:HALF], identity[:, 0:HALF])
-        nc.vector.tensor_copy(spread_cos[:, HALF:P], identity[:, 0:HALF])
-        nc.vector.tensor_scalar_mul(spread_sin[:, 0:HALF], identity[:, HALF:P], -1.0)
-        nc.vector.tensor_copy(spread_sin[:, HALF:P], identity[:, HALF:P])
-        cos_ps = spread.tile([P, TOKENS], FP32, name="cos_ps")
-        nc.tensor.matmul(cos_ps[:], lhsT=spread_cos[:], rhs=tables[:], start=True, stop=True)
-        sin_ps = spread.tile([P, TOKENS], FP32, name="sin_ps")
-        nc.tensor.matmul(sin_ps[:], lhsT=spread_sin[:], rhs=tables[:], start=True, stop=True)
-        cos_both = held.tile([P, TOKENS], FP32, name="cos_both")
-        nc.scalar.copy(cos_both[:], cos_ps[:])
-        signed_sin = held.tile([P, TOKENS], FP32, name="signed_sin")
-        nc.scalar.copy(signed_sin[:], sin_ps[:])
+        identity_cut = identity[:].rearrange("p (d t) -> p t d", t=CUTS)
+        pick = [held.tile([P, P], FP32, name=f"pick{t}") for t in range(CUTS)]
+        for t in range(CUTS):
+            for lower in (0, HALF):
+                nc.gpsimd.tensor_copy(pick[t][:, lower : lower + HALF], identity_cut[:, t, :])
+
+        with tc.psum_pool(name="spread", bufs=1) as spread:
+            nc.vector.tensor_copy(bias_rows[:, P : P + HALF], bias_rows[:, 0:HALF])
+            bias_ps = spread.tile([P, 2 * HEADS], FP32, name="bias_ps")
+            for partner in range(2):
+                nc.tensor.matmul(
+                    bias_ps[:, partner * HEADS : (partner + 1) * HEADS],
+                    lhsT=bias_rows[:, partner * HALF : partner * HALF + P],
+                    rhs=identity[0:HEADS, 0:HEADS],
+                    start=True,
+                    stop=True,
+                )
+            bias = held.tile([P, 2 * HEADS], FP32, name="bias")
+            nc.vector.tensor_copy(bias[:], bias_ps[:])
+
+            cos_ps = spread.tile([P, TOKENS], FP32, name="cos_ps")
+            sin_ps = spread.tile([P, TOKENS], FP32, name="sin_ps")
+            for table_ps, table_cut in ((cos_ps, cos_cut), (sin_ps, sin_cut)):
+                for t in range(CUTS):
+                    nc.tensor.matmul(
+                        table_ps[:, t * CUT_TOKENS : (t + 1) * CUT_TOKENS],
+                        lhsT=pick[t][:],
+                        rhs=table_cut[:],
+                        start=True,
+                        stop=True,
+                    )
+            cos_both = held.tile([P, TOKENS], FP32, name="cos_both")
+            nc.scalar.copy(cos_both[:], cos_ps[:])
+            signed_sin = held.tile([P, TOKENS], FP32, name="signed_sin")
+            nc.scalar.mul(signed_sin[0:HALF, :], sin_ps[0:HALF, :], -1.0)
+            nc.scalar.copy(signed_sin[HALF:P, :], sin_ps[HALF:P, :])
 
         w_partner = held.tile([P, K_STEPS, CHANNELS], BF16, name="w_partner")
         own_halves = w_own[:].rearrange("p k (h t d) -> p k h t d", t=2, d=HALF)
@@ -83,35 +93,36 @@ def tile_flashshellattention_kernel(tc, x, w_k, b_k, cos, sin, base, offs, out):
         for t in range(2):
             nc.vector.tensor_copy(partner_halves[:, :, :, t, :], own_halves[:, :, :, 1 - t, :])
 
-        for h in range(HEADS):
-            head = slice(h * P, (h + 1) * P)
-            own_ps = projections.tile([P, TOKENS], FP32, name="own_ps")
-            partner_ps = projections.tile([P, TOKENS], FP32, name="partner_ps")
-            for psum, weights in ((own_ps, w_own), (partner_ps, w_partner)):
-                for k in range(K_STEPS):
-                    nc.tensor.matmul(
-                        psum[:],
-                        lhsT=weights[:, k, head],
-                        rhs=x_sb[:, k, :],
-                        start=(k == 0),
-                        stop=(k == K_STEPS - 1),
-                    )
+        with tc.psum_pool(name="projections", bufs=2) as projections:
+            for h in range(HEADS):
+                head = slice(h * P, (h + 1) * P)
+                own_ps = projections.tile([P, TOKENS], FP32, name="own_ps")
+                partner_ps = projections.tile([P, TOKENS], FP32, name="partner_ps")
+                for psum, weights in ((own_ps, w_own), (partner_ps, w_partner)):
+                    for k in range(K_STEPS):
+                        nc.tensor.matmul(
+                            psum[:],
+                            lhsT=weights[:, k, head],
+                            rhs=x_sb[:, k, :],
+                            start=(k == 0),
+                            stop=(k == K_STEPS - 1),
+                        )
 
-            cos_part = products.tile([P, TOKENS], FP32, name="cos_part")
-            nc.vector.scalar_tensor_tensor(
-                cos_part[:], own_ps[:], bias[:, h : h + 1], cos_both[:], op0=ADD, op1=MULT
-            )
-            sin_part = products.tile([P, TOKENS], FP32, name="sin_part")
-            nc.vector.scalar_tensor_tensor(
-                sin_part[:],
-                partner_ps[:],
-                bias[:, HEADS + h : HEADS + h + 1],
-                signed_sin[:],
-                op0=ADD,
-                op1=MULT,
-            )
+                cos_part = products.tile([P, TOKENS], FP32, name="cos_part")
+                nc.vector.scalar_tensor_tensor(
+                    cos_part[:], own_ps[:], bias[:, h : h + 1], cos_both[:], op0=ADD, op1=MULT
+                )
+                sin_part = products.tile([P, TOKENS], FP32, name="sin_part")
+                nc.vector.scalar_tensor_tensor(
+                    sin_part[:],
+                    partner_ps[:],
+                    bias[:, HEADS + h : HEADS + h + 1],
+                    signed_sin[:],
+                    op0=ADD,
+                    op1=MULT,
+                )
 
-            nc.vector.tensor_tensor(
-                windows[h][:].indirect(offsets[:]), cos_part[:], sin_part[:], ADD
-            )
-            nc.sync.dma_start(out[head, :], windows[h][:])
+                nc.vector.tensor_tensor(
+                    windows[h][:].indirect(offsets[:]), cos_part[:], sin_part[:], ADD
+                )
+                nc.sync.dma_start(out[head, :], windows[h][:])

@@ -56,6 +56,10 @@ def tile_flashshellattention_kernel(tc, x, w_k, b_k, cos, sin, base, offs, out):
             for lower in (0, HALF):
                 nc.gpsimd.tensor_copy(pick[t][:, lower : lower + HALF], identity_cut[:, t, :])
 
+        sign = held.tile([P, 1], FP32, name="sign")
+        nc.gpsimd.memset(sign[0:HALF, :], -1.0)
+        nc.gpsimd.memset(sign[HALF:P, :], 1.0)
+
         with tc.psum_pool(name="spread", bufs=1) as spread:
             nc.vector.tensor_copy(bias_rows[:, P : P + HALF], bias_rows[:, 0:HALF])
             bias_ps = spread.tile([P, 2 * HEADS], FP32, name="bias_ps")
@@ -84,8 +88,7 @@ def tile_flashshellattention_kernel(tc, x, w_k, b_k, cos, sin, base, offs, out):
             cos_both = held.tile([P, TOKENS], FP32, name="cos_both")
             nc.scalar.copy(cos_both[:], cos_ps[:])
             signed_sin = held.tile([P, TOKENS], FP32, name="signed_sin")
-            nc.scalar.mul(signed_sin[0:HALF, :], sin_ps[0:HALF, :], -1.0)
-            nc.scalar.copy(signed_sin[HALF:P, :], sin_ps[HALF:P, :])
+            nc.vector.tensor_scalar_mul(signed_sin[:], sin_ps[:], sign[:, 0:1])
 
         w_partner = held.tile([P, K_STEPS, CHANNELS], BF16, name="w_partner")
         own_halves = w_own[:].rearrange("p k (h t d) -> p k h t d", t=2, d=HALF)

@@ -27,24 +27,26 @@ def tile_flashshellattention_kernel(tc, x, w_k, b_k, cos, sin, base, offs, out):
         tc.tile_pool(name="held", bufs=1) as held,
         tc.tile_pool(name="products", bufs=2) as products,
     ):
-        offsets = held.tile([P, TOKENS // 16], U16, name="offsets")
-        nc.sync.dma_start(offsets[:], offs)
+
+        x_sb = held.tile([P, K_STEPS, TOKENS], BF16, name="x_sb")
+        nc.sync.dma_start(x_sb[:], x.rearrange("(p k) n -> p k n", k=K_STEPS))
+
+        bias_rows = held.tile([HEADS, P + HALF], FP32, name="bias_rows")
+        nc.scalar.dma_start(bias_rows[:, 0:P], b_k.rearrange("(h c) o -> h (c o)", c=P))
 
         cos_cut = held.tile([P, CUT_TOKENS], FP32, name="cos_cut")
         nc.sync.dma_start(cos_cut[:], cos.rearrange("d (t n) -> (d t) n", t=CUTS))
         sin_cut = held.tile([P, CUT_TOKENS], FP32, name="sin_cut")
         nc.sync.dma_start(sin_cut[:], sin.rearrange("d (t n) -> (d t) n", t=CUTS))
 
-        bias_rows = held.tile([HEADS, P + HALF], FP32, name="bias_rows")
-        nc.scalar.dma_start(bias_rows[:, 0:P], b_k.rearrange("(h c) o -> h (c o)", c=P))
-
-        x_sb = held.tile([P, K_STEPS, TOKENS], BF16, name="x_sb")
-        nc.sync.dma_start(x_sb[:], x.rearrange("(p k) n -> p k n", k=K_STEPS))
         w_own = held.tile([P, K_STEPS, CHANNELS], BF16, name="w_own")
         nc.sync.dma_start(w_own[:], w_k.rearrange("(p k) c -> p k c", k=K_STEPS))
 
         windows = [held.tile([P, SLOTS], FP32, name=f"window{h}") for h in range(HEADS)]
-        for h in range(HEADS):
+        nc.sync.dma_start(windows[0][:], base[0:P, :])
+        offsets = held.tile([P, TOKENS // 16], U16, name="offsets")
+        nc.sync.dma_start(offsets[:], offs)
+        for h in range(1, HEADS):
             nc.sync.dma_start(windows[h][:], base[h * P : (h + 1) * P, :])
 
         identity = held.tile([P, P], FP32, name="identity")

@@ -130,4 +130,4 @@ def tile_flashshellattention_kernel(tc, x, w_k, b_k, cos, sin, base, offs, out):
                 nc.vector.tensor_tensor(
                     windows[h][:].indirect(offsets[:]), cos_part[:], sin_part[:], ADD
                 )
-                nc.sync.dma_start(out[head, :], windows[h][:])
+                nc.scalar.dma_start(out[head, :], windows[h][:])

@@ -1,3 +1,5 @@
+from contextlib import ExitStack
+
 import concourse.mybir as mybir
 from concourse.masks import make_identity
 
@@ -26,6 +28,7 @@ def tile_flashshellattention_kernel(tc, x, w_k, b_k, cos, sin, base, offs, out):
     with (
         tc.tile_pool(name="held", bufs=1) as held,
         tc.tile_pool(name="products", bufs=2) as products,
+        ExitStack() as tables,
     ):
 
         x_sb = held.tile([P, K_STEPS, TOKENS], BF16, name="x_sb")
@@ -62,9 +65,10 @@ def tile_flashshellattention_kernel(tc, x, w_k, b_k, cos, sin, base, offs, out):
         nc.gpsimd.memset(sign[0:HALF, :], -1.0)
         nc.gpsimd.memset(sign[HALF:P, :], 1.0)
 
-        with tc.psum_pool(name="spread", bufs=1) as spread:
+        spread = tables.enter_context(tc.psum_pool(name="spread", bufs=1))
+        with tc.psum_pool(name="bias_turned", bufs=1) as bias_turned:
             nc.vector.tensor_copy(bias_rows[:, P : P + HALF], bias_rows[:, 0:HALF])
-            bias_ps = spread.tile([P, 2 * HEADS], FP32, name="bias_ps")
+            bias_ps = bias_turned.tile([P, 2 * HEADS], FP32, name="bias_ps")
             for partner in range(2):
                 nc.tensor.matmul(
                     bias_ps[:, partner * HEADS : (partner + 1) * HEADS],

@@ -16,8 +16,7 @@ HIDDEN = 512
 K_STEPS = HIDDEN // P
 CHANNELS = HEADS * P
 TOKENS = 256
-CUTS = 2
-CUT_TOKENS = TOKENS // CUTS
+TABLE_ROW = 32
 SLOTS = 2048
 
 FLOPS = 2 * HIDDEN * CHANNELS * TOKENS
@@ -37,10 +36,11 @@ def tile_flashshellattention_kernel(tc, x, w_k, b_k, cos, sin, base, offs, out):
         bias_rows = held.tile([HEADS, P + HALF], FP32, name="bias_rows")
         nc.scalar.dma_start(bias_rows[:, 0:P], b_k.rearrange("(h c) o -> h (c o)", c=P))
 
-        cos_cut = held.tile([P, CUT_TOKENS], FP32, name="cos_cut")
-        nc.sync.dma_start(cos_cut[:], cos.rearrange("d (t n) -> (d t) n", t=CUTS))
-        sin_cut = held.tile([P, CUT_TOKENS], FP32, name="sin_cut")
-        nc.sync.dma_start(sin_cut[:], sin.rearrange("d (t n) -> (d t) n", t=CUTS))
+        table_rows = held.tile([P, 2, TOKENS], FP32, name="table_rows")
+        nc.vector.memset(table_rows[0:TABLE_ROW, :, :], 0.0)
+        nc.vector.memset(table_rows[TABLE_ROW + HALF : P, :, :], 0.0)
+        for i, table in enumerate((cos, sin)):
+            nc.sync.dma_start(table_rows[TABLE_ROW : TABLE_ROW + HALF, i, :], table)
 
         w_own = held.tile([P, K_STEPS, CHANNELS], BF16, name="w_own")
         nc.sync.dma_start(w_own[:], w_k.rearrange("(p k) c -> p k c", k=K_STEPS))
@@ -55,11 +55,11 @@ def tile_flashshellattention_kernel(tc, x, w_k, b_k, cos, sin, base, offs, out):
         identity = held.tile([P, P], FP32, name="identity")
         make_identity(nc, identity[:])
 
-        identity_cut = identity[:].rearrange("p (d t) -> p t d", t=CUTS)
-        pick = [held.tile([P, P], FP32, name=f"pick{t}") for t in range(CUTS)]
-        for t in range(CUTS):
-            for lower in (0, HALF):
-                nc.gpsimd.tensor_copy(pick[t][:, lower : lower + HALF], identity_cut[:, t, :])
+        pick = held.tile([P, P], FP32, name="pick")
+        for lower in (0, HALF):
+            nc.gpsimd.tensor_copy(
+                pick[:, lower : lower + HALF], identity[:, TABLE_ROW : TABLE_ROW + HALF]
+            )
 
         sign = held.tile([P, 1], FP32, name="sign")
         nc.gpsimd.memset(sign[0:HALF, :], -1.0)
@@ -82,15 +82,10 @@ def tile_flashshellattention_kernel(tc, x, w_k, b_k, cos, sin, base, offs, out):
 
             cos_ps = spread.tile([P, TOKENS], FP32, name="cos_ps")
             sin_ps = spread.tile([P, TOKENS], FP32, name="sin_ps")
-            for table_ps, table_cut in ((cos_ps, cos_cut), (sin_ps, sin_cut)):
-                for t in range(CUTS):
-                    nc.tensor.matmul(
-                        table_ps[:, t * CUT_TOKENS : (t + 1) * CUT_TOKENS],
-                        lhsT=pick[t][:],
-                        rhs=table_cut[:],
-                        start=True,
-                        stop=True,
-                    )
+            for i, table_ps in enumerate((cos_ps, sin_ps)):
+                nc.tensor.matmul(
+                    table_ps[:], lhsT=pick[:], rhs=table_rows[:, i, :], start=True, stop=True
+                )
             cos_both = held.tile([P, TOKENS], FP32, name="cos_both")
             nc.scalar.copy(cos_both[:], cos_ps[:])
             signed_sin = held.tile([P, TOKENS], FP32, name="signed_sin")

@@ -129,4 +129,4 @@ def tile_flashshellattention_kernel(tc, x, w_k, b_k, cos, sin, base, offs, out):
                 nc.vector.tensor_tensor(
                     windows[h][:].indirect(offsets[:]), cos_part[:], sin_part[:], ADD
                 )
-                nc.scalar.dma_start(out[head, :], windows[h][:])
+                nc.sync.dma_start(out[head, :], windows[h][:])

@@ -18,6 +18,7 @@ CHANNELS = HEADS * P
 TOKENS = 256
 TABLE_ROW = 32
 SLOTS = 2048
+DMA_ALIGN = 256
 
 FLOPS = 2 * HIDDEN * CHANNELS * TOKENS
 
@@ -30,22 +31,25 @@ def tile_flashshellattention_kernel(tc, x, w_k, b_k, cos, sin, base, offs, out):
         ExitStack() as tables,
     ):
 
-        x_sb = held.tile([P, K_STEPS, TOKENS], BF16, name="x_sb")
+        x_sb = held.tile([P, K_STEPS, TOKENS], BF16, name="x_sb", align_bytes=DMA_ALIGN)
         nc.sync.dma_start(x_sb[:], x.rearrange("(p k) n -> p k n", k=K_STEPS))
 
-        bias_rows = held.tile([HEADS, P + HALF], FP32, name="bias_rows")
-        nc.scalar.dma_start(bias_rows[:, 0:P], b_k.rearrange("(h c) o -> h (c o)", c=P))
-
-        table_rows = held.tile([P, 2, TOKENS], FP32, name="table_rows")
+        table_rows = held.tile([P, 2, TOKENS], FP32, name="table_rows", align_bytes=DMA_ALIGN)
         nc.vector.memset(table_rows[0:TABLE_ROW, :, :], 0.0)
         nc.vector.memset(table_rows[TABLE_ROW + HALF : P, :, :], 0.0)
         for i, table in enumerate((cos, sin)):
             nc.sync.dma_start(table_rows[TABLE_ROW : TABLE_ROW + HALF, i, :], table)
 
-        w_own = held.tile([P, K_STEPS, CHANNELS], BF16, name="w_own")
+        bias_rows = held.tile([HEADS, P + HALF], FP32, name="bias_rows")
+        nc.sync.dma_start(bias_rows[:, 0:P], b_k.rearrange("(h c) o -> h (c o)", c=P))
+
+        w_own = held.tile([P, K_STEPS, CHANNELS], BF16, name="w_own", align_bytes=DMA_ALIGN)
         nc.sync.dma_start(w_own[:], w_k.rearrange("(p k) c -> p k c", k=K_STEPS))
 
-        windows = [held.tile([P, SLOTS], FP32, name=f"window{h}") for h in range(HEADS)]
+        windows = [
+            held.tile([P, SLOTS], FP32, name=f"window{h}", align_bytes=DMA_ALIGN)
+            for h in range(HEADS)
+        ]
         nc.sync.dma_start(windows[0][:], base[0:P, :])
         offsets = held.tile([P, TOKENS // 16], U16, name="offsets")
         nc.sync.dma_start(offsets[:], offs)
@@ -55,15 +59,13 @@ def tile_flashshellattention_kernel(tc, x, w_k, b_k, cos, sin, base, offs, out):
         identity = held.tile([P, P], FP32, name="identity")
         make_identity(nc, identity[:])
 
-        pick = held.tile([P, P], FP32, name="pick")
-        for lower in (0, HALF):
-            nc.gpsimd.tensor_copy(
-                pick[:, lower : lower + HALF], identity[:, TABLE_ROW : TABLE_ROW + HALF]
-            )
-
-        sign = held.tile([P, 1], FP32, name="sign")
-        nc.gpsimd.memset(sign[0:HALF, :], -1.0)
-        nc.gpsimd.memset(sign[HALF:P, :], 1.0)
+        table_identity = identity[:, TABLE_ROW : TABLE_ROW + HALF]
+        pick_cos = held.tile([P, P], FP32, name="pick_cos")
+        pick_sin = held.tile([P, P], FP32, name="pick_sin")
+        nc.gpsimd.tensor_copy(pick_cos[:, 0:HALF], table_identity)
+        nc.gpsimd.tensor_copy(pick_cos[:, HALF:P], table_identity)
+        nc.gpsimd.tensor_scalar_mul(pick_sin[:, 0:HALF], table_identity, -1.0)
+        nc.gpsimd.tensor_copy(pick_sin[:, HALF:P], table_identity)
 
         spread = tables.enter_context(tc.psum_pool(name="spread", bufs=1))
         with tc.psum_pool(name="bias_turned", bufs=1) as bias_turned:
@@ -80,16 +82,15 @@ def tile_flashshellattention_kernel(tc, x, w_k, b_k, cos, sin, base, offs, out):
             bias = held.tile([P, 2 * HEADS], FP32, name="bias")
             nc.vector.tensor_copy(bias[:], bias_ps[:])
 
-            cos_ps = spread.tile([P, TOKENS], FP32, name="cos_ps")
-            sin_ps = spread.tile([P, TOKENS], FP32, name="sin_ps")
-            for i, table_ps in enumerate((cos_ps, sin_ps)):
+            tables_ps = spread.tile([P, 2, TOKENS], FP32, name="tables_ps")
+            for i, pick in enumerate((pick_cos, pick_sin)):
                 nc.tensor.matmul(
-                    table_ps[:], lhsT=pick[:], rhs=table_rows[:, i, :], start=True, stop=True
+                    tables_ps[:, i, :], lhsT=pick[:], rhs=table_rows[:, i, :], start=True, stop=True
                 )
-            cos_both = held.tile([P, TOKENS], FP32, name="cos_both")
-            nc.scalar.copy(cos_both[:], cos_ps[:])
-            signed_sin = held.tile([P, TOKENS], FP32, name="signed_sin")
-            nc.vector.tensor_scalar_mul(signed_sin[:], sin_ps[:], sign[:, 0:1])
+            tables_sb = held.tile([P, 2, TOKENS], FP32, name="tables_sb")
+            nc.vector.tensor_copy(tables_sb[:], tables_ps[:])
+            cos_both = tables_sb[:, 0, :]
+            signed_sin = tables_sb[:, 1, :]
 
         w_partner = held.tile([P, K_STEPS, CHANNELS], BF16, name="w_partner")
         own_halves = w_own[:].rearrange("p k (h t d) -> p k h t d", t=2, d=HALF)
@@ -114,14 +115,14 @@ def tile_flashshellattention_kernel(tc, x, w_k, b_k, cos, sin, base, offs, out):
 
                 cos_part = products.tile([P, TOKENS], FP32, name="cos_part")
                 nc.vector.scalar_tensor_tensor(
-                    cos_part[:], own_ps[:], bias[:, h : h + 1], cos_both[:], op0=ADD, op1=MULT
+                    cos_part[:], own_ps[:], bias[:, h : h + 1], cos_both, op0=ADD, op1=MULT
                 )
                 sin_part = products.tile([P, TOKENS], FP32, name="sin_part")
                 nc.vector.scalar_tensor_tensor(
                     sin_part[:],
                     partner_ps[:],
                     bias[:, HEADS + h : HEADS + h + 1],
-                    signed_sin[:],
+                    signed_sin,
                     op0=ADD,
                     op1=MULT,
                 )

@@ -18,7 +18,7 @@ CHANNELS = HEADS * P
 TOKENS = 256
 TABLE_ROW = 32
 SLOTS = 2048
-DMA_ALIGN = 256
+DMA_ALIGN = 4096
 
 FLOPS = 2 * HIDDEN * CHANNELS * TOKENS
 

from contextlib import ExitStack

import concourse.mybir as mybir
from concourse.masks import make_identity

FP32 = mybir.dt.float32
BF16 = mybir.dt.bfloat16
U16 = mybir.dt.uint16
ADD = mybir.AluOpType.add
MULT = mybir.AluOpType.mult

P = 128
HALF = 64
HEADS = 4
HIDDEN = 512
K_STEPS = HIDDEN // P
CHANNELS = HEADS * P
TOKENS = 256
TABLE_ROW = 32
SLOTS = 2048
DMA_ALIGN = 4096

FLOPS = 2 * HIDDEN * CHANNELS * TOKENS


def tile_flashshellattention_kernel(tc, x, w_k, b_k, cos, sin, base, offs, out):
    nc = tc.nc
    with (
        tc.tile_pool(name="held", bufs=1) as held,
        tc.tile_pool(name="products", bufs=2) as products,
        ExitStack() as tables,
    ):

        x_sb = held.tile([P, K_STEPS, TOKENS], BF16, name="x_sb", align_bytes=DMA_ALIGN)
        nc.sync.dma_start(x_sb[:], x.rearrange("(p k) n -> p k n", k=K_STEPS))

        table_rows = held.tile([P, 2, TOKENS], FP32, name="table_rows", align_bytes=DMA_ALIGN)
        nc.vector.memset(table_rows[0:TABLE_ROW, :, :], 0.0)
        nc.vector.memset(table_rows[TABLE_ROW + HALF : P, :, :], 0.0)
        for i, table in enumerate((cos, sin)):
            nc.sync.dma_start(table_rows[TABLE_ROW : TABLE_ROW + HALF, i, :], table)

        bias_rows = held.tile([HEADS, P + HALF], FP32, name="bias_rows")
        nc.sync.dma_start(bias_rows[:, 0:P], b_k.rearrange("(h c) o -> h (c o)", c=P))

        w_own = held.tile([P, K_STEPS, CHANNELS], BF16, name="w_own", align_bytes=DMA_ALIGN)
        nc.sync.dma_start(w_own[:], w_k.rearrange("(p k) c -> p k c", k=K_STEPS))

        windows = [
            held.tile([P, SLOTS], FP32, name=f"window{h}", align_bytes=DMA_ALIGN)
            for h in range(HEADS)
        ]
        nc.sync.dma_start(windows[0][:], base[0:P, :])
        offsets = held.tile([P, TOKENS // 16], U16, name="offsets")
        nc.sync.dma_start(offsets[:], offs)
        for h in range(1, HEADS):
            nc.sync.dma_start(windows[h][:], base[h * P : (h + 1) * P, :])

        identity = held.tile([P, P], FP32, name="identity")
        make_identity(nc, identity[:])

        table_identity = identity[:, TABLE_ROW : TABLE_ROW + HALF]
        pick_cos = held.tile([P, P], FP32, name="pick_cos")
        pick_sin = held.tile([P, P], FP32, name="pick_sin")
        nc.gpsimd.tensor_copy(pick_cos[:, 0:HALF], table_identity)
        nc.gpsimd.tensor_copy(pick_cos[:, HALF:P], table_identity)
        nc.gpsimd.tensor_scalar_mul(pick_sin[:, 0:HALF], table_identity, -1.0)
        nc.gpsimd.tensor_copy(pick_sin[:, HALF:P], table_identity)

        spread = tables.enter_context(tc.psum_pool(name="spread", bufs=1))
        with tc.psum_pool(name="bias_turned", bufs=1) as bias_turned:
            nc.vector.tensor_copy(bias_rows[:, P : P + HALF], bias_rows[:, 0:HALF])
            bias_ps = bias_turned.tile([P, 2 * HEADS], FP32, name="bias_ps")
            for partner in range(2):
                nc.tensor.matmul(
                    bias_ps[:, partner * HEADS : (partner + 1) * HEADS],
                    lhsT=bias_rows[:, partner * HALF : partner * HALF + P],
                    rhs=identity[0:HEADS, 0:HEADS],
                    start=True,
                    stop=True,
                )
            bias = held.tile([P, 2 * HEADS], FP32, name="bias")
            nc.vector.tensor_copy(bias[:], bias_ps[:])

            tables_ps = spread.tile([P, 2, TOKENS], FP32, name="tables_ps")
            for i, pick in enumerate((pick_cos, pick_sin)):
                nc.tensor.matmul(
                    tables_ps[:, i, :], lhsT=pick[:], rhs=table_rows[:, i, :], start=True, stop=True
                )
            tables_sb = held.tile([P, 2, TOKENS], FP32, name="tables_sb")
            nc.vector.tensor_copy(tables_sb[:], tables_ps[:])
            cos_both = tables_sb[:, 0, :]
            signed_sin = tables_sb[:, 1, :]

        w_partner = held.tile([P, K_STEPS, CHANNELS], BF16, name="w_partner")
        own_halves = w_own[:].rearrange("p k (h t d) -> p k h t d", t=2, d=HALF)
        partner_halves = w_partner[:].rearrange("p k (h t d) -> p k h t d", t=2, d=HALF)
        for t in range(2):
            nc.vector.tensor_copy(partner_halves[:, :, :, t, :], own_halves[:, :, :, 1 - t, :])

        with tc.psum_pool(name="projections", bufs=2) as projections:
            for h in range(HEADS):
                head = slice(h * P, (h + 1) * P)
                own_ps = projections.tile([P, TOKENS], FP32, name="own_ps")
                partner_ps = projections.tile([P, TOKENS], FP32, name="partner_ps")
                for psum, weights in ((own_ps, w_own), (partner_ps, w_partner)):
                    for k in range(K_STEPS):
                        nc.tensor.matmul(
                            psum[:],
                            lhsT=weights[:, k, head],
                            rhs=x_sb[:, k, :],
                            start=(k == 0),
                            stop=(k == K_STEPS - 1),
                        )

                cos_part = products.tile([P, TOKENS], FP32, name="cos_part")
                nc.vector.scalar_tensor_tensor(
                    cos_part[:], own_ps[:], bias[:, h : h + 1], cos_both, op0=ADD, op1=MULT
                )
                sin_part = products.tile([P, TOKENS], FP32, name="sin_part")
                nc.vector.scalar_tensor_tensor(
                    sin_part[:],
                    partner_ps[:],
                    bias[:, HEADS + h : HEADS + h + 1],
                    signed_sin,
                    op0=ADD,
                    op1=MULT,
                )

                nc.vector.tensor_tensor(
                    windows[h][:].indirect(offsets[:]), cos_part[:], sin_part[:], ADD
                )
                nc.sync.dma_start(out[head, :], windows[h][:])
